import numpy as np
import ml_dtypes


def mxq(x, axis, fmt="e4m3"):
    dtype, down = {"e4m3": (ml_dtypes.float8_e4m3fn, 7), "e5m2": (ml_dtypes.float8_e5m2, 14)}[fmt]
    v = np.moveaxis(np.asarray(x, np.float32).astype(ml_dtypes.bfloat16).astype(np.float64), axis, -1)
    blocks = v.reshape(v.shape[:-1] + (-1, 32))
    amax = np.abs(blocks).max(-1, keepdims=True)
    byte = np.maximum(np.where(amax > 0, np.frexp(amax)[1] - 1 + 127, 0) - down, 1)
    scale = np.exp2(byte - 127.0)
    codes = (blocks / scale).astype(np.float32).astype(dtype).astype(np.float64)
    return np.moveaxis((codes * scale).reshape(v.shape), -1, axis)


WIDE = False


def mx_kscale(k):
    if not WIDE:
        return np.ones(k)
    levels = np.array([10, -10, 5, -5, 0])
    a = np.random.permutation(np.resize(levels, k // 512 * 4)).reshape(k // 512, 4)
    idx = np.arange(k)
    return np.exp2(a[idx // 512, idx % 128 // 32])


BF16 = ml_dtypes.bfloat16


def bf(x):
    return np.asarray(x, np.float32).astype(BF16)


def f64(x):
    return np.asarray(x).astype(np.float64)


N, E, HD, H1, H3, DM = 16384, 512, 256, 1024, 128, 1024
C = 2 * HD


def setup_inputs():
    s = mx_kscale(N)
    t = mx_kscale(C)
    r = np.concatenate([np.full(HD, 2.0 / np.sqrt(HD)), np.full(HD, 8.0 / np.sqrt(N * HD))])
    return {
        "H_A": bf(np.random.standard_normal((N, E)) * 0.25 * s[:, None]),
        "H_mean_A": bf(np.random.standard_normal((N, HD)) * 0.35 / s[:, None] * t[HD:]),
        "H_mean_M": bf(np.random.standard_normal((E, HD)) * 0.35 * t[:HD]),
        "wEA1": bf(np.random.standard_normal((C, H3)) * (r / t)[:, None]),
        "bEA1": bf(np.random.standard_normal(H3) * 0.1),
    }


def reference(H_A, H_mean_A, H_mean_M, wEA1, bEA1):
    sum_A = mxq(f64(H_A), 0, "e4m3").T @ mxq(f64(H_mean_A), 0, "e4m3")
    EventA = np.concatenate([f64(H_mean_M), sum_A], axis=1)
    return np.maximum((mxq(EventA, 1, "e4m3") @ mxq(f64(wEA1), 0, "e4m3")) + f64(bEA1), 0.0)

@@ -1,0 +1,171 @@
+import concourse.mybir as mybir
+from concourse.masks import make_identity
+
+BF16 = mybir.dt.bfloat16
+F32 = mybir.dt.float32
+U32 = mybir.dt.uint32
+U8 = mybir.dt.uint8
+FP8X4 = mybir.dt.float8_e4m3fn_x4
+ADD = mybir.AluOpType.add
+
+P = 128
+PACK = 4
+K_PASS = P * PACK
+
+NODES, EVENTS, HD, H3 = 16384, 512, 256, 128
+FUSED = 2 * HD
+HD_TILES = HD // P
+EVENT_TILES = EVENTS // P
+
+CHUNK_PASSES = 2
+CHUNK_NODES = CHUNK_PASSES * K_PASS
+CHUNKS = NODES // CHUNK_NODES
+
+SCALAR_COLS = 384
+
+RUN = 4
+
+FLOPS = 2 * NODES * EVENTS * HD + 2 * EVENTS * FUSED * H3
+
+
+def regroup(copy, grouped, rows):
+    copy(
+        out=grouped.rearrange("p (c i) j -> p c j i", i=RUN),
+        in_=rows.rearrange("p j (c i) -> p c j i", i=RUN),
+    )
+
+
+def regroup_passes(copy, grouped, rows):
+    copy(
+        out=grouped.rearrange("p n (c i) j -> p n c j i", i=RUN),
+        in_=rows.rearrange("p n j (c i) -> p n c j i", i=RUN),
+    )
+
+
+def tile_mymodel_icdm_pa_k_kernel(tc, H_A, H_mean_A, H_mean_M, wEA1, bEA1, out):
+    nc = tc.nc
+    with tc.tile_pool(name="consts", bufs=1) as consts, tc.tile_pool(name="raw", bufs=8) as raw, tc.tile_pool(
+        name="work", bufs=3
+    ) as work, tc.psum_pool(name="psum", bufs=1) as psum:
+        events_own = consts.tile([P, EVENT_TILES, HD], BF16)
+        nc.scalar.dma_start(out=events_own[:], in_=H_mean_M.rearrange("(a p) c -> p a c", p=P))
+        w_rows = consts.tile([P, PACK, H3], BF16)
+        nc.scalar.dma_start(out=w_rows[:], in_=wEA1.rearrange("(j p) h -> p j h", p=P))
+        bias_rows = consts.tile([P, H3], BF16)
+        nc.vector.memset(bias_rows[:], 0.0)
+        nc.scalar.dma_start(out=bias_rows[0:1, :], in_=bEA1.rearrange("(o h) -> o h", o=1))
+
+        identity = consts.tile([P, P], BF16)
+        make_identity(nc, identity[:])
+        ones = consts.tile([P, P], BF16)
+        nc.vector.memset(ones[:], 1.0)
+
+        fused_rows = consts.tile([P, PACK, EVENTS], BF16)
+
+        own_t = psum.tile([P, HD_TILES, EVENTS], BF16)
+        for j in range(HD_TILES):
+            for a in range(EVENT_TILES):
+                nc.tensor.transpose(
+                    own_t[:, j, a * P : (a + 1) * P], events_own[:, a, j * P : (j + 1) * P], identity[:]
+                )
+        nc.scalar.copy(out=fused_rows[:, 0:HD_TILES, :], in_=own_t[:])
+
+        bias_ps = psum.tile([P, H3], F32)
+        nc.tensor.matmul(out=bias_ps[:], lhsT=ones[:], rhs=bias_rows[:], start=True, stop=True)
+        bias_all = consts.tile([P, H3], F32)
+        nc.vector.tensor_copy(out=bias_all[:], in_=bias_ps[:])
+
+        w_grouped = consts.tile([P, H3, PACK], BF16, align_bytes=64)
+        regroup(nc.vector.tensor_copy, w_grouped[:], w_rows[:])
+        w_codes = consts.tile([P, H3], U32, align_bytes=64)
+        w_scales = consts.tile([P, H3], U8, align_bytes=64)
+        nc.vector.quantize_mx(
+            out=w_codes[:].bitcast(FP8X4), scales=w_scales[:], in_=w_grouped[:].rearrange("p h j -> p (h j)")
+        )
+
+        sum_t = [psum.tile([P, EVENTS], F32, name="sum_t%d" % m) for m in range(HD_TILES)]
+
+        def load_and_regroup(i):
+            nodes = slice(i * CHUNK_NODES, (i + 1) * CHUNK_NODES)
+            ha_rows = raw.tile([P, CHUNK_PASSES, PACK, EVENTS], BF16)
+            nc.sync.dma_start(
+                out=ha_rows[:].rearrange("p n j e -> p n (j e)"),
+                in_=H_A[nodes, :].rearrange("(n p j) e -> p n (j e)", p=P, j=PACK),
+            )
+            hm_rows = raw.tile([P, CHUNK_PASSES, PACK, HD], BF16)
+            nc.sync.dma_start(
+                out=hm_rows[:].rearrange("p n j d -> p n (j d)"),
+                in_=H_mean_A[nodes, :].rearrange("(n p j) d -> p n (j d)", p=P, j=PACK),
+            )
+            ha_grouped = work.tile([P, CHUNK_PASSES, EVENTS, PACK], BF16, align_bytes=64)
+            hm_grouped = work.tile([P, CHUNK_PASSES, HD, PACK], BF16, align_bytes=64)
+            for n in range(CHUNK_PASSES):
+                regroup(nc.scalar.copy, ha_grouped[:, n, 0:SCALAR_COLS, :], ha_rows[:, n, :, 0:SCALAR_COLS])
+            regroup_passes(nc.vector.tensor_copy, hm_grouped[:], hm_rows[:])
+            regroup_passes(
+                nc.vector.tensor_copy, ha_grouped[:, :, SCALAR_COLS:EVENTS, :], ha_rows[:, :, :, SCALAR_COLS:EVENTS]
+            )
+            return ha_grouped, hm_grouped
+
+        def quantise_and_multiply(i, ha_grouped, hm_grouped):
+            ha_codes = work.tile([P, CHUNK_PASSES, EVENTS], U32, align_bytes=64)
+            ha_scales = work.tile([P, CHUNK_PASSES, EVENTS], U8, align_bytes=64)
+            nc.vector.quantize_mx(
+                out=ha_codes[:].rearrange("p n e -> p (n e)").bitcast(FP8X4),
+                scales=ha_scales[:].rearrange("p n e -> p (n e)"),
+                in_=ha_grouped[:].rearrange("p n e j -> p (n e j)"),
+            )
+            hm_codes = work.tile([P, CHUNK_PASSES, HD], U32, align_bytes=64)
+            hm_scales = work.tile([P, CHUNK_PASSES, HD], U8, align_bytes=64)
+            nc.vector.quantize_mx(
+                out=hm_codes[:].rearrange("p n d -> p (n d)").bitcast(FP8X4),
+                scales=hm_scales[:].rearrange("p n d -> p (n d)"),
+                in_=hm_grouped[:].rearrange("p n d j -> p (n d j)"),
+            )
+            for n in range(CHUNK_PASSES):
+                for m in range(HD_TILES):
+                    nc.tensor.matmul_mx(
+                        out=sum_t[m][:],
+                        lhsT=hm_codes[:, n, m * P : (m + 1) * P].bitcast(FP8X4),
+                        lhsT_scale=hm_scales[:, n, m * P : (m + 1) * P],
+                        rhs=ha_codes[:, n, :].bitcast(FP8X4),
+                        rhs_scale=ha_scales[:, n, :],
+                        start=(i == 0 and n == 0),
+                        stop=(i == CHUNKS - 1 and n == CHUNK_PASSES - 1),
+                    )
+
+        grouped = load_and_regroup(0)
+        for i in range(1, CHUNKS):
+            grouped_next = load_and_regroup(i)
+            quantise_and_multiply(i - 1, grouped[0], grouped[1])
+            grouped = grouped_next
+        quantise_and_multiply(CHUNKS - 1, grouped[0], grouped[1])
+
+        nc.vector.tensor_copy(out=fused_rows[:, HD_TILES, :], in_=sum_t[0][:])
+        nc.scalar.copy(out=fused_rows[:, HD_TILES + 1, :], in_=sum_t[1][:])
+        fused_grouped = consts.tile([P, EVENTS, PACK], BF16, align_bytes=64)
+        regroup(nc.vector.tensor_copy, fused_grouped[:], fused_rows[:])
+        fused_codes = consts.tile([P, EVENTS], U32, align_bytes=64)
+        fused_scales = consts.tile([P, EVENTS], U8, align_bytes=64)
+        nc.vector.quantize_mx(
+            out=fused_codes[:].bitcast(FP8X4),
+            scales=fused_scales[:],
+            in_=fused_grouped[:].rearrange("p e j -> p (e j)"),
+        )
+        out_ps = psum.tile([P, EVENT_TILES, H3], F32)
+        for a in range(EVENT_TILES):
+            nc.tensor.matmul_mx(
+                out=out_ps[:, a, :],
+                lhsT=fused_codes[:, a * P : (a + 1) * P].bitcast(FP8X4),
+                lhsT_scale=fused_scales[:, a * P : (a + 1) * P],
+                rhs=w_codes[:].bitcast(FP8X4),
+                rhs_scale=w_scales[:],
+                start=True,
+                stop=True,
+            )
+        result = consts.tile([P, EVENT_TILES, H3], F32)
+        nc.vector.tensor_tensor(
+            out=result[:], in0=out_ps[:], in1=bias_all[:].unsqueeze(1).to_broadcast([P, EVENT_TILES, H3]), op=ADD
+        )
+        nc.vector.tensor_scalar_max(out=result[:], in0=result[:], scalar1=0.0)
+        nc.sync.dma_start(out=out.rearrange("(a p) h -> p a h", p=P), in_=result[:])

@@ -1,3 +1,5 @@
+from contextlib import ExitStack
+
 import concourse.mybir as mybir
 from concourse.masks import make_identity
 
@@ -25,6 +27,9 @@ SCALAR_COLS = 384
 
 RUN = 4
 
+RAW_BUFS = 8
+WORK_BUFS = 3
+
 FLOPS = 2 * NODES * EVENTS * HD + 2 * EVENTS * FUSED * H3
 
 
@@ -44,24 +49,41 @@ def regroup_passes(copy, grouped, rows):
 
 def tile_mymodel_icdm_pa_k_kernel(tc, H_A, H_mean_A, H_mean_M, wEA1, bEA1, out):
     nc = tc.nc
-    with tc.tile_pool(name="consts", bufs=1) as consts, tc.tile_pool(name="raw", bufs=8) as raw, tc.tile_pool(
-        name="work", bufs=3
-    ) as work, tc.psum_pool(name="psum", bufs=1) as psum:
-        events_own = consts.tile([P, EVENT_TILES, HD], BF16)
-        nc.scalar.dma_start(out=events_own[:], in_=H_mean_M.rearrange("(a p) c -> p a c", p=P))
+    with ExitStack() as stack:
+        consts = stack.enter_context(tc.tile_pool(name="consts", bufs=1))
+        raw = stack.enter_context(tc.tile_pool(name="raw", bufs=RAW_BUFS))
+        work = stack.enter_context(tc.tile_pool(name="work", bufs=WORK_BUFS))
+        psum = stack.enter_context(tc.psum_pool(name="psum", bufs=1))
+        stack.enter_context(tc.manual_schedule())
+
         w_rows = consts.tile([P, PACK, H3], BF16)
-        nc.scalar.dma_start(out=w_rows[:], in_=wEA1.rearrange("(j p) h -> p j h", p=P))
+        nc.sync.dma_start(out=w_rows[:], in_=wEA1.rearrange("(j p) h -> p j h", p=P))
         bias_rows = consts.tile([P, H3], BF16)
         nc.vector.memset(bias_rows[:], 0.0)
-        nc.scalar.dma_start(out=bias_rows[0:1, :], in_=bEA1.rearrange("(o h) -> o h", o=1))
+        nc.sync.dma_start(out=bias_rows[0:1, :], in_=bEA1.rearrange("(o h) -> o h", o=1))
+        events_own = consts.tile([P, EVENT_TILES, HD], BF16)
+        nc.sync.dma_start(out=events_own[:], in_=H_mean_M.rearrange("(a p) c -> p a c", p=P))
 
         identity = consts.tile([P, P], BF16)
         make_identity(nc, identity[:])
         ones = consts.tile([P, P], BF16)
         nc.vector.memset(ones[:], 1.0)
 
-        fused_rows = consts.tile([P, PACK, EVENTS], BF16)
+        w_grouped = consts.tile([P, H3, PACK], BF16, align_bytes=64)
+        regroup(nc.vector.tensor_copy, w_grouped[:], w_rows[:])
 
+        bias_ps = psum.tile([P, H3], F32)
+        nc.tensor.matmul(out=bias_ps[:], lhsT=ones[:], rhs=bias_rows[:], start=True, stop=True)
+        bias_all = consts.tile([P, H3], F32)
+        nc.vector.tensor_copy(out=bias_all[:], in_=bias_ps[:])
+
+        w_codes = consts.tile([P, H3], U32, align_bytes=64)
+        w_scales = consts.tile([P, H3], U8, align_bytes=64)
+        nc.vector.quantize_mx(
+            out=w_codes[:].bitcast(FP8X4), scales=w_scales[:], in_=w_grouped[:].rearrange("p h j -> p (h j)")
+        )
+
+        fused_rows = consts.tile([P, PACK, EVENTS], BF16)
         own_t = psum.tile([P, HD_TILES, EVENTS], BF16)
         for j in range(HD_TILES):
             for a in range(EVENT_TILES):
@@ -70,33 +92,22 @@ def tile_mymodel_icdm_pa_k_kernel(tc, H_A, H_mean_A, H_mean_M, wEA1, bEA1, out):
                 )
         nc.scalar.copy(out=fused_rows[:, 0:HD_TILES, :], in_=own_t[:])
 
-        bias_ps = psum.tile([P, H3], F32)
-        nc.tensor.matmul(out=bias_ps[:], lhsT=ones[:], rhs=bias_rows[:], start=True, stop=True)
-        bias_all = consts.tile([P, H3], F32)
-        nc.vector.tensor_copy(out=bias_all[:], in_=bias_ps[:])
-
-        w_grouped = consts.tile([P, H3, PACK], BF16, align_bytes=64)
-        regroup(nc.vector.tensor_copy, w_grouped[:], w_rows[:])
-        w_codes = consts.tile([P, H3], U32, align_bytes=64)
-        w_scales = consts.tile([P, H3], U8, align_bytes=64)
-        nc.vector.quantize_mx(
-            out=w_codes[:].bitcast(FP8X4), scales=w_scales[:], in_=w_grouped[:].rearrange("p h j -> p (h j)")
-        )
-
         sum_t = [psum.tile([P, EVENTS], F32, name="sum_t%d" % m) for m in range(HD_TILES)]
 
         def load_and_regroup(i):
-            nodes = slice(i * CHUNK_NODES, (i + 1) * CHUNK_NODES)
+            first = i * CHUNK_NODES
             ha_rows = raw.tile([P, CHUNK_PASSES, PACK, EVENTS], BF16)
-            nc.sync.dma_start(
-                out=ha_rows[:].rearrange("p n j e -> p n (j e)"),
-                in_=H_A[nodes, :].rearrange("(n p j) e -> p n (j e)", p=P, j=PACK),
-            )
             hm_rows = raw.tile([P, CHUNK_PASSES, PACK, HD], BF16)
-            nc.sync.dma_start(
-                out=hm_rows[:].rearrange("p n j d -> p n (j d)"),
-                in_=H_mean_A[nodes, :].rearrange("(n p j) d -> p n (j d)", p=P, j=PACK),
-            )
+            for n in range(CHUNK_PASSES):
+                nodes = slice(first + n * K_PASS, first + (n + 1) * K_PASS)
+                nc.sync.dma_start(
+                    out=ha_rows[:, n].rearrange("p j e -> p (j e)"),
+                    in_=H_A[nodes, :].rearrange("(p j) e -> p (j e)", j=PACK),
+                )
+                nc.sync.dma_start(
+                    out=hm_rows[:, n].rearrange("p j d -> p (j d)"),
+                    in_=H_mean_A[nodes, :].rearrange("(p j) d -> p (j d)", j=PACK),
+                )
             ha_grouped = work.tile([P, CHUNK_PASSES, EVENTS, PACK], BF16, align_bytes=64)
             hm_grouped = work.tile([P, CHUNK_PASSES, HD, PACK], BF16, align_bytes=64)
             for n in range(CHUNK_PASSES):
@@ -107,14 +118,7 @@ def tile_mymodel_icdm_pa_k_kernel(tc, H_A, H_mean_A, H_mean_M, wEA1, bEA1, out):
             )
             return ha_grouped, hm_grouped
 
-        def quantise_and_multiply(i, ha_grouped, hm_grouped):
-            ha_codes = work.tile([P, CHUNK_PASSES, EVENTS], U32, align_bytes=64)
-            ha_scales = work.tile([P, CHUNK_PASSES, EVENTS], U8, align_bytes=64)
-            nc.vector.quantize_mx(
-                out=ha_codes[:].rearrange("p n e -> p (n e)").bitcast(FP8X4),
-                scales=ha_scales[:].rearrange("p n e -> p (n e)"),
-                in_=ha_grouped[:].rearrange("p n e j -> p (n e j)"),
-            )
+        def quantise_features(hm_grouped):
             hm_codes = work.tile([P, CHUNK_PASSES, HD], U32, align_bytes=64)
             hm_scales = work.tile([P, CHUNK_PASSES, HD], U8, align_bytes=64)
             nc.vector.quantize_mx(
@@ -122,24 +126,38 @@ def tile_mymodel_icdm_pa_k_kernel(tc, H_A, H_mean_A, H_mean_M, wEA1, bEA1, out):
                 scales=hm_scales[:].rearrange("p n d -> p (n d)"),
                 in_=hm_grouped[:].rearrange("p n d j -> p (n d j)"),
             )
-            for n in range(CHUNK_PASSES):
-                for m in range(HD_TILES):
-                    nc.tensor.matmul_mx(
-                        out=sum_t[m][:],
-                        lhsT=hm_codes[:, n, m * P : (m + 1) * P].bitcast(FP8X4),
-                        lhsT_scale=hm_scales[:, n, m * P : (m + 1) * P],
-                        rhs=ha_codes[:, n, :].bitcast(FP8X4),
-                        rhs_scale=ha_scales[:, n, :],
-                        start=(i == 0 and n == 0),
-                        stop=(i == CHUNKS - 1 and n == CHUNK_PASSES - 1),
-                    )
+            return hm_codes, hm_scales
 
-        grouped = load_and_regroup(0)
-        for i in range(1, CHUNKS):
-            grouped_next = load_and_regroup(i)
-            quantise_and_multiply(i - 1, grouped[0], grouped[1])
-            grouped = grouped_next
-        quantise_and_multiply(CHUNKS - 1, grouped[0], grouped[1])
+        def multiply_pass(i, n, ha_grouped, hm_codes, hm_scales):
+            ha_codes = work.tile([P, EVENTS], U32, align_bytes=64)
+            ha_scales = work.tile([P, EVENTS], U8, align_bytes=64)
+            nc.vector.quantize_mx(
+                out=ha_codes[:].bitcast(FP8X4),
+                scales=ha_scales[:],
+                in_=ha_grouped[:, n].rearrange("p e j -> p (e j)"),
+            )
+            for m in range(HD_TILES):
+                nc.tensor.matmul_mx(
+                    out=sum_t[m][:],
+                    lhsT=hm_codes[:, n, m * P : (m + 1) * P].bitcast(FP8X4),
+                    lhsT_scale=hm_scales[:, n, m * P : (m + 1) * P],
+                    rhs=ha_codes[:].bitcast(FP8X4),
+                    rhs_scale=ha_scales[:],
+                    start=(i == 0 and n == 0),
+                    stop=(i == CHUNKS - 1 and n == CHUNK_PASSES - 1),
+                )
+
+        LAST = CHUNK_PASSES - 1
+        held = None
+        for i in range(CHUNKS):
+            ha_grouped, hm_grouped = load_and_regroup(i)
+            if held is not None:
+                multiply_pass(i - 1, LAST, held[0], held[1], held[2])
+            hm_codes, hm_scales = quantise_features(hm_grouped)
+            for n in range(LAST):
+                multiply_pass(i, n, ha_grouped, hm_codes, hm_scales)
+            held = (ha_grouped, hm_codes, hm_scales)
+        multiply_pass(CHUNKS - 1, LAST, held[0], held[1], held[2])
 
         nc.vector.tensor_copy(out=fused_rows[:, HD_TILES, :], in_=sum_t[0][:])
         nc.scalar.copy(out=fused_rows[:, HD_TILES + 1, :], in_=sum_t[1][:])

@@ -23,7 +23,7 @@ CHUNK_PASSES = 2
 CHUNK_NODES = CHUNK_PASSES * K_PASS
 CHUNKS = NODES // CHUNK_NODES
 
-SCALAR_COLS = 384
+SCALAR_COLS = 416
 
 RUN = 4
 
@@ -61,8 +61,6 @@ def tile_mymodel_icdm_pa_k_kernel(tc, H_A, H_mean_A, H_mean_M, wEA1, bEA1, out):
         bias_rows = consts.tile([P, H3], BF16)
         nc.vector.memset(bias_rows[:], 0.0)
         nc.sync.dma_start(out=bias_rows[0:1, :], in_=bEA1.rearrange("(o h) -> o h", o=1))
-        events_own = consts.tile([P, EVENT_TILES, HD], BF16)
-        nc.sync.dma_start(out=events_own[:], in_=H_mean_M.rearrange("(a p) c -> p a c", p=P))
 
         identity = consts.tile([P, P], BF16)
         make_identity(nc, identity[:])
@@ -83,31 +81,20 @@ def tile_mymodel_icdm_pa_k_kernel(tc, H_A, H_mean_A, H_mean_M, wEA1, bEA1, out):
             out=w_codes[:].bitcast(FP8X4), scales=w_scales[:], in_=w_grouped[:].rearrange("p h j -> p (h j)")
         )
 
-        fused_rows = consts.tile([P, PACK, EVENTS], BF16)
-        own_t = psum.tile([P, HD_TILES, EVENTS], BF16)
-        for j in range(HD_TILES):
-            for a in range(EVENT_TILES):
-                nc.tensor.transpose(
-                    own_t[:, j, a * P : (a + 1) * P], events_own[:, a, j * P : (j + 1) * P], identity[:]
-                )
-        nc.scalar.copy(out=fused_rows[:, 0:HD_TILES, :], in_=own_t[:])
-
         sum_t = [psum.tile([P, EVENTS], F32, name="sum_t%d" % m) for m in range(HD_TILES)]
 
         def load_and_regroup(i):
-            first = i * CHUNK_NODES
+            nodes = slice(i * CHUNK_NODES, (i + 1) * CHUNK_NODES)
             ha_rows = raw.tile([P, CHUNK_PASSES, PACK, EVENTS], BF16)
+            nc.sync.dma_start(
+                out=ha_rows[:].rearrange("p n j e -> p n (j e)"),
+                in_=H_A[nodes, :].rearrange("(n p j) e -> p n (j e)", p=P, j=PACK),
+            )
             hm_rows = raw.tile([P, CHUNK_PASSES, PACK, HD], BF16)
-            for n in range(CHUNK_PASSES):
-                nodes = slice(first + n * K_PASS, first + (n + 1) * K_PASS)
-                nc.sync.dma_start(
-                    out=ha_rows[:, n].rearrange("p j e -> p (j e)"),
-                    in_=H_A[nodes, :].rearrange("(p j) e -> p (j e)", j=PACK),
-                )
-                nc.sync.dma_start(
-                    out=hm_rows[:, n].rearrange("p j d -> p (j d)"),
-                    in_=H_mean_A[nodes, :].rearrange("(p j) d -> p (j d)", j=PACK),
-                )
+            nc.sync.dma_start(
+                out=hm_rows[:].rearrange("p n j d -> p n (j d)"),
+                in_=H_mean_A[nodes, :].rearrange("(n p j) d -> p n (j d)", p=P, j=PACK),
+            )
             ha_grouped = work.tile([P, CHUNK_PASSES, EVENTS, PACK], BF16, align_bytes=64)
             hm_grouped = work.tile([P, CHUNK_PASSES, HD, PACK], BF16, align_bytes=64)
             for n in range(CHUNK_PASSES):
@@ -126,14 +113,14 @@ def tile_mymodel_icdm_pa_k_kernel(tc, H_A, H_mean_A, H_mean_M, wEA1, bEA1, out):
                 scales=hm_scales[:].rearrange("p n d -> p (n d)"),
                 in_=hm_grouped[:].rearrange("p n d j -> p (n d j)"),
             )
-            return hm_codes, hm_scales
+            ha_codes = work.tile([P, CHUNK_PASSES, EVENTS], U32, align_bytes=64)
+            ha_scales = work.tile([P, CHUNK_PASSES, EVENTS], U8, align_bytes=64)
+            return hm_codes, hm_scales, ha_codes, ha_scales
 
-        def multiply_pass(i, n, ha_grouped, hm_codes, hm_scales):
-            ha_codes = work.tile([P, EVENTS], U32, align_bytes=64)
-            ha_scales = work.tile([P, EVENTS], U8, align_bytes=64)
+        def multiply_pass(i, n, ha_grouped, hm_codes, hm_scales, ha_codes, ha_scales):
             nc.vector.quantize_mx(
-                out=ha_codes[:].bitcast(FP8X4),
-                scales=ha_scales[:],
+                out=ha_codes[:, n].bitcast(FP8X4),
+                scales=ha_scales[:, n],
                 in_=ha_grouped[:, n].rearrange("p e j -> p (e j)"),
             )
             for m in range(HD_TILES):
@@ -141,23 +128,35 @@ def tile_mymodel_icdm_pa_k_kernel(tc, H_A, H_mean_A, H_mean_M, wEA1, bEA1, out):
                     out=sum_t[m][:],
                     lhsT=hm_codes[:, n, m * P : (m + 1) * P].bitcast(FP8X4),
                     lhsT_scale=hm_scales[:, n, m * P : (m + 1) * P],
-                    rhs=ha_codes[:].bitcast(FP8X4),
-                    rhs_scale=ha_scales[:],
+                    rhs=ha_codes[:, n].bitcast(FP8X4),
+                    rhs_scale=ha_scales[:, n],
                     start=(i == 0 and n == 0),
                     stop=(i == CHUNKS - 1 and n == CHUNK_PASSES - 1),
                 )
 
         LAST = CHUNK_PASSES - 1
-        held = None
+        operands = None
         for i in range(CHUNKS):
             ha_grouped, hm_grouped = load_and_regroup(i)
-            if held is not None:
-                multiply_pass(i - 1, LAST, held[0], held[1], held[2])
-            hm_codes, hm_scales = quantise_features(hm_grouped)
+            if i == 0:
+                events_own = consts.tile([P, EVENT_TILES, HD], BF16)
+                nc.sync.dma_start(out=events_own[:], in_=H_mean_M.rearrange("(a p) c -> p a c", p=P))
+            else:
+                multiply_pass(i - 1, LAST, *operands)
+            operands = (ha_grouped,) + quantise_features(hm_grouped)
             for n in range(LAST):
-                multiply_pass(i, n, ha_grouped, hm_codes, hm_scales)
-            held = (ha_grouped, hm_codes, hm_scales)
-        multiply_pass(CHUNKS - 1, LAST, held[0], held[1], held[2])
+                multiply_pass(i, n, *operands)
+
+        fused_rows = consts.tile([P, PACK, EVENTS], BF16)
+        own_t = psum.tile([P, HD_TILES, EVENTS], BF16)
+        for j in range(HD_TILES):
+            for a in range(EVENT_TILES):
+                nc.tensor.transpose(
+                    own_t[:, j, a * P : (a + 1) * P], events_own[:, a, j * P : (j + 1) * P], identity[:]
+                )
+        nc.scalar.copy(out=fused_rows[:, 0:HD_TILES, :], in_=own_t[:])
+
+        multiply_pass(CHUNKS - 1, LAST, *operands)
 
         nc.vector.tensor_copy(out=fused_rows[:, HD_TILES, :], in_=sum_t[0][:])
         nc.scalar.copy(out=fused_rows[:, HD_TILES + 1, :], in_=sum_t[1][:])

@@ -18,17 +18,17 @@ NODES, EVENTS, HD, H3 = 16384, 512, 256, 128
 FUSED = 2 * HD
 HD_TILES = HD // P
 EVENT_TILES = EVENTS // P
+PASSES = NODES // K_PASS
 
-CHUNK_PASSES = 2
-CHUNK_NODES = CHUNK_PASSES * K_PASS
-CHUNKS = NODES // CHUNK_NODES
+ROUND_PASSES = 2
+ROUNDS = PASSES // ROUND_PASSES
 
-SCALAR_COLS = 416
+SCALAR_COLS = 320
 
 RUN = 4
 
-RAW_BUFS = 8
-WORK_BUFS = 3
+RAW_ROUNDS = 8
+WORK_ROUNDS = 3
 
 FLOPS = 2 * NODES * EVENTS * HD + 2 * EVENTS * FUSED * H3
 
@@ -51,132 +51,119 @@ def tile_mymodel_icdm_pa_k_kernel(tc, H_A, H_mean_A, H_mean_M, wEA1, bEA1, out):
     nc = tc.nc
     with ExitStack() as stack:
         consts = stack.enter_context(tc.tile_pool(name="consts", bufs=1))
-        raw = stack.enter_context(tc.tile_pool(name="raw", bufs=RAW_BUFS))
-        work = stack.enter_context(tc.tile_pool(name="work", bufs=WORK_BUFS))
+        raw_pass = stack.enter_context(tc.tile_pool(name="raw_pass", bufs=RAW_ROUNDS * ROUND_PASSES))
+        raw_round = stack.enter_context(tc.tile_pool(name="raw_round", bufs=RAW_ROUNDS))
+        work_pass = stack.enter_context(tc.tile_pool(name="work_pass", bufs=WORK_ROUNDS * ROUND_PASSES))
+        work_round = stack.enter_context(tc.tile_pool(name="work_round", bufs=WORK_ROUNDS))
         psum = stack.enter_context(tc.psum_pool(name="psum", bufs=1))
         stack.enter_context(tc.manual_schedule())
 
-        w_rows = consts.tile([P, PACK, H3], BF16)
-        nc.sync.dma_start(out=w_rows[:], in_=wEA1.rearrange("(j p) h -> p j h", p=P))
-        bias_rows = consts.tile([P, H3], BF16)
-        nc.vector.memset(bias_rows[:], 0.0)
-        nc.sync.dma_start(out=bias_rows[0:1, :], in_=bEA1.rearrange("(o h) -> o h", o=1))
+        def quantise(pool, name, grouped):
+            words = grouped.shape[1] // PACK
+            codes = pool.tile([P, words], U32, name=name + "_codes", tag=name + "_codes", align_bytes=64)
+            scales = pool.tile([P, words], U8, name=name + "_scales", tag=name + "_scales", align_bytes=64)
+            nc.vector.quantize_mx(out=codes[:].bitcast(FP8X4), scales=scales[:], in_=grouped)
+            return codes, scales
 
         identity = consts.tile([P, P], BF16)
         make_identity(nc, identity[:])
         ones = consts.tile([P, P], BF16)
         nc.vector.memset(ones[:], 1.0)
+        bias_rows = consts.tile([P, H3], BF16)
+        nc.vector.memset(bias_rows[:], 0.0)
 
+        sum_t = [psum.tile([P, EVENTS], F32, name="sum_t%d" % m) for m in range(HD_TILES)]
+
+        def load_events(t):
+            ha_rows = raw_pass.tile([P, PACK, EVENTS], BF16)
+            nc.sync.dma_start(
+                out=ha_rows[:].rearrange("p j e -> p (j e)"),
+                in_=H_A[t * K_PASS : (t + 1) * K_PASS, :].rearrange("(p j) e -> p (j e)", j=PACK),
+            )
+            return ha_rows
+
+        def load_features(t):
+            hm_rows = raw_round.tile([P, ROUND_PASSES, PACK, HD], BF16)
+            nc.sync.dma_start(
+                out=hm_rows[:].rearrange("p n j d -> p n (j d)"),
+                in_=H_mean_A[t * K_PASS : (t + ROUND_PASSES) * K_PASS, :].rearrange(
+                    "(n p j) d -> p n (j d)", p=P, j=PACK
+                ),
+            )
+            return hm_rows
+
+        def multiply(t, ha_codes, ha_scales, hm_codes, hm_scales):
+            first = (t % ROUND_PASSES) * HD
+            for m in range(HD_TILES):
+                features = slice(first + m * P, first + (m + 1) * P)
+                nc.tensor.matmul_mx(
+                    out=sum_t[m][:],
+                    lhsT=hm_codes[:, features].bitcast(FP8X4),
+                    lhsT_scale=hm_scales[:, features],
+                    rhs=ha_codes[:].bitcast(FP8X4),
+                    rhs_scale=ha_scales[:],
+                    start=(t == 0),
+                    stop=(t == PASSES - 1),
+                )
+
+        for r in range(ROUNDS):
+            t = r * ROUND_PASSES
+            ha_rows_a = load_events(t)
+            hm_rows = load_features(t)
+            ha_rows_b = load_events(t + 1)
+
+            ha_grouped_a = work_pass.tile([P, EVENTS, PACK], BF16, tag="ha_grouped", align_bytes=64)
+            regroup(nc.scalar.copy, ha_grouped_a[:], ha_rows_a[:])
+            ha_grouped_b = work_pass.tile([P, EVENTS, PACK], BF16, tag="ha_grouped", align_bytes=64)
+            regroup(nc.scalar.copy, ha_grouped_b[:, 0:SCALAR_COLS, :], ha_rows_b[:, :, 0:SCALAR_COLS])
+
+            hm_grouped = work_round.tile([P, ROUND_PASSES, HD, PACK], BF16, align_bytes=64)
+            regroup_passes(nc.vector.tensor_copy, hm_grouped[:], hm_rows[:])
+            ha_a = quantise(work_pass, "ha", ha_grouped_a[:].rearrange("p e j -> p (e j)"))
+            regroup(nc.vector.tensor_copy, ha_grouped_b[:, SCALAR_COLS:EVENTS, :], ha_rows_b[:, :, SCALAR_COLS:EVENTS])
+            hm = quantise(work_round, "hm", hm_grouped[:].rearrange("p n d j -> p (n d j)"))
+            multiply(t, ha_a[0], ha_a[1], hm[0], hm[1])
+
+            if r == ROUNDS - 1:
+                events_own = consts.tile([P, EVENT_TILES, HD], BF16)
+                nc.sync.dma_start(out=events_own[:], in_=H_mean_M.rearrange("(a p) c -> p a c", p=P))
+                w_rows = consts.tile([P, PACK, H3], BF16)
+                nc.sync.dma_start(out=w_rows[:], in_=wEA1.rearrange("(j p) h -> p j h", p=P))
+                nc.sync.dma_start(out=bias_rows[0:1, :], in_=bEA1.rearrange("(o h) -> o h", o=1))
+                own_t = psum.tile([P, HD_TILES, EVENTS], BF16)
+                for j in range(HD_TILES):
+                    for a in range(EVENT_TILES):
+                        nc.tensor.transpose(
+                            own_t[:, j, a * P : (a + 1) * P], events_own[:, a, j * P : (j + 1) * P], identity[:]
+                        )
+                fused_rows = consts.tile([P, PACK, EVENTS], BF16)
+                nc.scalar.copy(out=fused_rows[:, 0:HD_TILES, :], in_=own_t[:])
+
+            ha_b = quantise(work_pass, "ha", ha_grouped_b[:].rearrange("p e j -> p (e j)"))
+            multiply(t + 1, ha_b[0], ha_b[1], hm[0], hm[1])
+
+        nc.vector.tensor_copy(out=fused_rows[:, HD_TILES, :], in_=sum_t[0][:])
+        nc.scalar.copy(out=fused_rows[:, HD_TILES + 1, :], in_=sum_t[1][:])
+        fused_grouped = consts.tile([P, EVENTS, PACK], BF16, align_bytes=64)
+        regroup(nc.vector.tensor_copy, fused_grouped[:], fused_rows[:])
         w_grouped = consts.tile([P, H3, PACK], BF16, align_bytes=64)
-        regroup(nc.vector.tensor_copy, w_grouped[:], w_rows[:])
+        regroup(nc.scalar.copy, w_grouped[:], w_rows[:])
+        w = quantise(consts, "w", w_grouped[:].rearrange("p h j -> p (h j)"))
+        fused = quantise(consts, "fused", fused_grouped[:].rearrange("p e j -> p (e j)"))
 
         bias_ps = psum.tile([P, H3], F32)
         nc.tensor.matmul(out=bias_ps[:], lhsT=ones[:], rhs=bias_rows[:], start=True, stop=True)
         bias_all = consts.tile([P, H3], F32)
         nc.vector.tensor_copy(out=bias_all[:], in_=bias_ps[:])
 
-        w_codes = consts.tile([P, H3], U32, align_bytes=64)
-        w_scales = consts.tile([P, H3], U8, align_bytes=64)
-        nc.vector.quantize_mx(
-            out=w_codes[:].bitcast(FP8X4), scales=w_scales[:], in_=w_grouped[:].rearrange("p h j -> p (h j)")
-        )
-
-        sum_t = [psum.tile([P, EVENTS], F32, name="sum_t%d" % m) for m in range(HD_TILES)]
-
-        def load_and_regroup(i):
-            nodes = slice(i * CHUNK_NODES, (i + 1) * CHUNK_NODES)
-            ha_rows = raw.tile([P, CHUNK_PASSES, PACK, EVENTS], BF16)
-            nc.sync.dma_start(
-                out=ha_rows[:].rearrange("p n j e -> p n (j e)"),
-                in_=H_A[nodes, :].rearrange("(n p j) e -> p n (j e)", p=P, j=PACK),
-            )
-            hm_rows = raw.tile([P, CHUNK_PASSES, PACK, HD], BF16)
-            nc.sync.dma_start(
-                out=hm_rows[:].rearrange("p n j d -> p n (j d)"),
-                in_=H_mean_A[nodes, :].rearrange("(n p j) d -> p n (j d)", p=P, j=PACK),
-            )
-            ha_grouped = work.tile([P, CHUNK_PASSES, EVENTS, PACK], BF16, align_bytes=64)
-            hm_grouped = work.tile([P, CHUNK_PASSES, HD, PACK], BF16, align_bytes=64)
-            for n in range(CHUNK_PASSES):
-                regroup(nc.scalar.copy, ha_grouped[:, n, 0:SCALAR_COLS, :], ha_rows[:, n, :, 0:SCALAR_COLS])
-            regroup_passes(nc.vector.tensor_copy, hm_grouped[:], hm_rows[:])
-            regroup_passes(
-                nc.vector.tensor_copy, ha_grouped[:, :, SCALAR_COLS:EVENTS, :], ha_rows[:, :, :, SCALAR_COLS:EVENTS]
-            )
-            return ha_grouped, hm_grouped
-
-        def quantise_features(hm_grouped):
-            hm_codes = work.tile([P, CHUNK_PASSES, HD], U32, align_bytes=64)
-            hm_scales = work.tile([P, CHUNK_PASSES, HD], U8, align_bytes=64)
-            nc.vector.quantize_mx(
-                out=hm_codes[:].rearrange("p n d -> p (n d)").bitcast(FP8X4),
-                scales=hm_scales[:].rearrange("p n d -> p (n d)"),
-                in_=hm_grouped[:].rearrange("p n d j -> p (n d j)"),
-            )
-            ha_codes = work.tile([P, CHUNK_PASSES, EVENTS], U32, align_bytes=64)
-            ha_scales = work.tile([P, CHUNK_PASSES, EVENTS], U8, align_bytes=64)
-            return hm_codes, hm_scales, ha_codes, ha_scales
-
-        def multiply_pass(i, n, ha_grouped, hm_codes, hm_scales, ha_codes, ha_scales):
-            nc.vector.quantize_mx(
-                out=ha_codes[:, n].bitcast(FP8X4),
-                scales=ha_scales[:, n],
-                in_=ha_grouped[:, n].rearrange("p e j -> p (e j)"),
-            )
-            for m in range(HD_TILES):
-                nc.tensor.matmul_mx(
-                    out=sum_t[m][:],
-                    lhsT=hm_codes[:, n, m * P : (m + 1) * P].bitcast(FP8X4),
-                    lhsT_scale=hm_scales[:, n, m * P : (m + 1) * P],
-                    rhs=ha_codes[:, n].bitcast(FP8X4),
-                    rhs_scale=ha_scales[:, n],
-                    start=(i == 0 and n == 0),
-                    stop=(i == CHUNKS - 1 and n == CHUNK_PASSES - 1),
-                )
-
-        LAST = CHUNK_PASSES - 1
-        operands = None
-        for i in range(CHUNKS):
-            ha_grouped, hm_grouped = load_and_regroup(i)
-            if i == 0:
-                events_own = consts.tile([P, EVENT_TILES, HD], BF16)
-                nc.sync.dma_start(out=events_own[:], in_=H_mean_M.rearrange("(a p) c -> p a c", p=P))
-            else:
-                multiply_pass(i - 1, LAST, *operands)
-            operands = (ha_grouped,) + quantise_features(hm_grouped)
-            for n in range(LAST):
-                multiply_pass(i, n, *operands)
-
-        fused_rows = consts.tile([P, PACK, EVENTS], BF16)
-        own_t = psum.tile([P, HD_TILES, EVENTS], BF16)
-        for j in range(HD_TILES):
-            for a in range(EVENT_TILES):
-                nc.tensor.transpose(
-                    own_t[:, j, a * P : (a + 1) * P], events_own[:, a, j * P : (j + 1) * P], identity[:]
-                )
-        nc.scalar.copy(out=fused_rows[:, 0:HD_TILES, :], in_=own_t[:])
-
-        multiply_pass(CHUNKS - 1, LAST, *operands)
-
-        nc.vector.tensor_copy(out=fused_rows[:, HD_TILES, :], in_=sum_t[0][:])
-        nc.scalar.copy(out=fused_rows[:, HD_TILES + 1, :], in_=sum_t[1][:])
-        fused_grouped = consts.tile([P, EVENTS, PACK], BF16, align_bytes=64)
-        regroup(nc.vector.tensor_copy, fused_grouped[:], fused_rows[:])
-        fused_codes = consts.tile([P, EVENTS], U32, align_bytes=64)
-        fused_scales = consts.tile([P, EVENTS], U8, align_bytes=64)
-        nc.vector.quantize_mx(
-            out=fused_codes[:].bitcast(FP8X4),
-            scales=fused_scales[:],
-            in_=fused_grouped[:].rearrange("p e j -> p (e j)"),
-        )
         out_ps = psum.tile([P, EVENT_TILES, H3], F32)
         for a in range(EVENT_TILES):
             nc.tensor.matmul_mx(
                 out=out_ps[:, a, :],
-                lhsT=fused_codes[:, a * P : (a + 1) * P].bitcast(FP8X4),
-                lhsT_scale=fused_scales[:, a * P : (a + 1) * P],
-                rhs=w_codes[:].bitcast(FP8X4),
-                rhs_scale=w_scales[:],
+                lhsT=fused[0][:, a * P : (a + 1) * P].bitcast(FP8X4),
+                lhsT_scale=fused[1][:, a * P : (a + 1) * P],
+                rhs=w[0][:].bitcast(FP8X4),
+                rhs_scale=w[1][:],
                 start=True,
                 stop=True,
             )

from contextlib import ExitStack

import concourse.mybir as mybir
from concourse.masks import make_identity

BF16 = mybir.dt.bfloat16
F32 = mybir.dt.float32
U32 = mybir.dt.uint32
U8 = mybir.dt.uint8
FP8X4 = mybir.dt.float8_e4m3fn_x4
ADD = mybir.AluOpType.add

P = 128
PACK = 4
K_PASS = P * PACK

NODES, EVENTS, HD, H3 = 16384, 512, 256, 128
FUSED = 2 * HD
HD_TILES = HD // P
EVENT_TILES = EVENTS // P
PASSES = NODES // K_PASS

ROUND_PASSES = 2
ROUNDS = PASSES // ROUND_PASSES

SCALAR_COLS = 320

RUN = 4

RAW_ROUNDS = 8
WORK_ROUNDS = 3

FLOPS = 2 * NODES * EVENTS * HD + 2 * EVENTS * FUSED * H3


def regroup(copy, grouped, rows):
    copy(
        out=grouped.rearrange("p (c i) j -> p c j i", i=RUN),
        in_=rows.rearrange("p j (c i) -> p c j i", i=RUN),
    )


def regroup_passes(copy, grouped, rows):
    copy(
        out=grouped.rearrange("p n (c i) j -> p n c j i", i=RUN),
        in_=rows.rearrange("p n j (c i) -> p n c j i", i=RUN),
    )


def tile_mymodel_icdm_pa_k_kernel(tc, H_A, H_mean_A, H_mean_M, wEA1, bEA1, out):
    nc = tc.nc
    with ExitStack() as stack:
        consts = stack.enter_context(tc.tile_pool(name="consts", bufs=1))
        raw_pass = stack.enter_context(tc.tile_pool(name="raw_pass", bufs=RAW_ROUNDS * ROUND_PASSES))
        raw_round = stack.enter_context(tc.tile_pool(name="raw_round", bufs=RAW_ROUNDS))
        work_pass = stack.enter_context(tc.tile_pool(name="work_pass", bufs=WORK_ROUNDS * ROUND_PASSES))
        work_round = stack.enter_context(tc.tile_pool(name="work_round", bufs=WORK_ROUNDS))
        psum = stack.enter_context(tc.psum_pool(name="psum", bufs=1))
        stack.enter_context(tc.manual_schedule())

        def quantise(pool, name, grouped):
            words = grouped.shape[1] // PACK
            codes = pool.tile([P, words], U32, name=name + "_codes", tag=name + "_codes", align_bytes=64)
            scales = pool.tile([P, words], U8, name=name + "_scales", tag=name + "_scales", align_bytes=64)
            nc.vector.quantize_mx(out=codes[:].bitcast(FP8X4), scales=scales[:], in_=grouped)
            return codes, scales

        identity = consts.tile([P, P], BF16)
        make_identity(nc, identity[:])
        ones = consts.tile([P, P], BF16)
        nc.vector.memset(ones[:], 1.0)
        bias_rows = consts.tile([P, H3], BF16)
        nc.vector.memset(bias_rows[:], 0.0)

        sum_t = [psum.tile([P, EVENTS], F32, name="sum_t%d" % m) for m in range(HD_TILES)]

        def load_events(t):
            ha_rows = raw_pass.tile([P, PACK, EVENTS], BF16)
            nc.sync.dma_start(
                out=ha_rows[:].rearrange("p j e -> p (j e)"),
                in_=H_A[t * K_PASS : (t + 1) * K_PASS, :].rearrange("(p j) e -> p (j e)", j=PACK),
            )
            return ha_rows

        def load_features(t):
            hm_rows = raw_round.tile([P, ROUND_PASSES, PACK, HD], BF16)
            nc.sync.dma_start(
                out=hm_rows[:].rearrange("p n j d -> p n (j d)"),
                in_=H_mean_A[t * K_PASS : (t + ROUND_PASSES) * K_PASS, :].rearrange(
                    "(n p j) d -> p n (j d)", p=P, j=PACK
                ),
            )
            return hm_rows

        def multiply(t, ha_codes, ha_scales, hm_codes, hm_scales):
            first = (t % ROUND_PASSES) * HD
            for m in range(HD_TILES):
                features = slice(first + m * P, first + (m + 1) * P)
                nc.tensor.matmul_mx(
                    out=sum_t[m][:],
                    lhsT=hm_codes[:, features].bitcast(FP8X4),
                    lhsT_scale=hm_scales[:, features],
                    rhs=ha_codes[:].bitcast(FP8X4),
                    rhs_scale=ha_scales[:],
                    start=(t == 0),
                    stop=(t == PASSES - 1),
                )

        for r in range(ROUNDS):
            t = r * ROUND_PASSES
            ha_rows_a = load_events(t)
            hm_rows = load_features(t)
            ha_rows_b = load_events(t + 1)

            ha_grouped_a = work_pass.tile([P, EVENTS, PACK], BF16, tag="ha_grouped", align_bytes=64)
            regroup(nc.scalar.copy, ha_grouped_a[:], ha_rows_a[:])
            ha_grouped_b = work_pass.tile([P, EVENTS, PACK], BF16, tag="ha_grouped", align_bytes=64)
            regroup(nc.scalar.copy, ha_grouped_b[:, 0:SCALAR_COLS, :], ha_rows_b[:, :, 0:SCALAR_COLS])

            hm_grouped = work_round.tile([P, ROUND_PASSES, HD, PACK], BF16, align_bytes=64)
            regroup_passes(nc.vector.tensor_copy, hm_grouped[:], hm_rows[:])
            ha_a = quantise(work_pass, "ha", ha_grouped_a[:].rearrange("p e j -> p (e j)"))
            regroup(nc.vector.tensor_copy, ha_grouped_b[:, SCALAR_COLS:EVENTS, :], ha_rows_b[:, :, SCALAR_COLS:EVENTS])
            hm = quantise(work_round, "hm", hm_grouped[:].rearrange("p n d j -> p (n d j)"))
            multiply(t, ha_a[0], ha_a[1], hm[0], hm[1])

            if r == ROUNDS - 1:
                events_own = consts.tile([P, EVENT_TILES, HD], BF16)
                nc.sync.dma_start(out=events_own[:], in_=H_mean_M.rearrange("(a p) c -> p a c", p=P))
                w_rows = consts.tile([P, PACK, H3], BF16)
                nc.sync.dma_start(out=w_rows[:], in_=wEA1.rearrange("(j p) h -> p j h", p=P))
                nc.sync.dma_start(out=bias_rows[0:1, :], in_=bEA1.rearrange("(o h) -> o h", o=1))
                own_t = psum.tile([P, HD_TILES, EVENTS], BF16)
                for j in range(HD_TILES):
                    for a in range(EVENT_TILES):
                        nc.tensor.transpose(
                            own_t[:, j, a * P : (a + 1) * P], events_own[:, a, j * P : (j + 1) * P], identity[:]
                        )
                fused_rows = consts.tile([P, PACK, EVENTS], BF16)
                nc.scalar.copy(out=fused_rows[:, 0:HD_TILES, :], in_=own_t[:])

            ha_b = quantise(work_pass, "ha", ha_grouped_b[:].rearrange("p e j -> p (e j)"))
            multiply(t + 1, ha_b[0], ha_b[1], hm[0], hm[1])

        nc.vector.tensor_copy(out=fused_rows[:, HD_TILES, :], in_=sum_t[0][:])
        nc.scalar.copy(out=fused_rows[:, HD_TILES + 1, :], in_=sum_t[1][:])
        fused_grouped = consts.tile([P, EVENTS, PACK], BF16, align_bytes=64)
        regroup(nc.vector.tensor_copy, fused_grouped[:], fused_rows[:])
        w_grouped = consts.tile([P, H3, PACK], BF16, align_bytes=64)
        regroup(nc.scalar.copy, w_grouped[:], w_rows[:])
        w = quantise(consts, "w", w_grouped[:].rearrange("p h j -> p (h j)"))
        fused = quantise(consts, "fused", fused_grouped[:].rearrange("p e j -> p (e j)"))

        bias_ps = psum.tile([P, H3], F32)
        nc.tensor.matmul(out=bias_ps[:], lhsT=ones[:], rhs=bias_rows[:], start=True, stop=True)
        bias_all = consts.tile([P, H3], F32)
        nc.vector.tensor_copy(out=bias_all[:], in_=bias_ps[:])

        out_ps = psum.tile([P, EVENT_TILES, H3], F32)
        for a in range(EVENT_TILES):
            nc.tensor.matmul_mx(
                out=out_ps[:, a, :],
                lhsT=fused[0][:, a * P : (a + 1) * P].bitcast(FP8X4),
                lhsT_scale=fused[1][:, a * P : (a + 1) * P],
                rhs=w[0][:].bitcast(FP8X4),
                rhs_scale=w[1][:],
                start=True,
                stop=True,
            )
        result = consts.tile([P, EVENT_TILES, H3], F32)
        nc.vector.tensor_tensor(
            out=result[:], in0=out_ps[:], in1=bias_all[:].unsqueeze(1).to_broadcast([P, EVENT_TILES, H3]), op=ADD
        )
        nc.vector.tensor_scalar_max(out=result[:], in0=result[:], scalar1=0.0)
        nc.sync.dma_start(out=out.rearrange("(a p) h -> p a h", p=P), in_=result[:])
